import numpy as np
import ml_dtypes


def mxq(x, axis, fmt="e4m3"):
    dtype, down = {"e4m3": (ml_dtypes.float8_e4m3fn, 7), "e5m2": (ml_dtypes.float8_e5m2, 14)}[fmt]
    v = np.moveaxis(np.asarray(x, np.float32).astype(ml_dtypes.bfloat16).astype(np.float64), axis, -1)
    blocks = v.reshape(v.shape[:-1] + (-1, 32))
    amax = np.abs(blocks).max(-1, keepdims=True)
    byte = np.maximum(np.where(amax > 0, np.frexp(amax)[1] - 1 + 127, 0) - down, 1)
    scale = np.exp2(byte - 127.0)
    codes = (blocks / scale).astype(np.float32).astype(dtype).astype(np.float64)
    return np.moveaxis((codes * scale).reshape(v.shape), -1, axis)


WIDE = False


def mx_kscale(k):
    if not WIDE:
        return np.ones(k)
    levels = np.array([10, -10, 5, -5, 0])
    a = np.random.permutation(np.resize(levels, k // 512 * 4)).reshape(k // 512, 4)
    idx = np.arange(k)
    return np.exp2(a[idx // 512, idx % 128 // 32])


BF16 = ml_dtypes.bfloat16


def bf(x):
    return np.asarray(x, np.float32).astype(BF16)


def f64(x):
    return np.asarray(x).astype(np.float64)


B, STOCH, ACT_DIM, HIDDEN, DETER = 8192, 384, 128, 512, 128
K1 = STOCH + ACT_DIM
EPS = 1e-4


def silu(v):
    return v / (1.0 + np.exp(-v))


def rmsnorm(v, w):
    return v * (1.0 / np.sqrt(np.mean(v * v, axis=-1, keepdims=True) + EPS)) * w


def setup_inputs():
    s = mx_kscale(K1)[:STOCH]
    w1 = np.random.standard_normal((HIDDEN, K1)) * 0.07 / np.sqrt(K1)
    w1[:, :STOCH] = w1[:, :STOCH] / s
    return {"stoch": bf(np.random.standard_normal((B, STOCH)) * s),
            "action": bf(np.random.standard_normal((B, ACT_DIM))),
            "tok_w1": bf(w1),
            "tok_b1": bf(np.random.standard_normal(HIDDEN) * 0.03),
            "tok_nw": bf(1.0 + 0.1 * np.random.standard_normal(HIDDEN)),
            "tok_w2": bf(np.random.standard_normal((DETER, HIDDEN)) * 1.5 / np.sqrt(HIDDEN)),
            "tok_b2": bf(np.random.standard_normal(DETER) * 0.2)}


def reference(stoch, action, tok_w1, tok_b1, tok_nw, tok_w2, tok_b2):
    act = f64(action)
    act = act / np.maximum(np.abs(act), 1.0)
    u = np.concatenate([f64(stoch), act], axis=-1)
    h = (mxq(u, 1, "e4m3") @ mxq(f64(tok_w1), 1, "e4m3").T) + f64(tok_b1)
    g = silu(rmsnorm(h, f64(tok_nw)))
    return (mxq(g, 1, "e4m3") @ mxq(f64(tok_w2), 1, "e4m3").T) + f64(tok_b2)

@@ -1,0 +1,188 @@
+import math
+from contextlib import ExitStack
+
+import concourse.mybir as mybir
+from concourse.masks import make_identity
+
+F32 = mybir.dt.float32
+BF16 = mybir.dt.bfloat16
+U32 = mybir.dt.uint32
+U8 = mybir.dt.uint8
+FP8X4 = mybir.dt.float8_e4m3fn_x4
+ALU = mybir.AluOpType
+ACT = mybir.ActivationFunctionType
+
+P = 128
+PACK = 4
+ROWS, STOCH, ACTION, HIDDEN, DETER = 8192, 384, 128, 512, 128
+K1 = STOCH + ACTION
+EPS = 1e-4
+TILES = 4
+GROUP = TILES * P
+GROUPS = ROWS // GROUP
+
+FLOPS = 2 * ROWS * K1 * HIDDEN + 2 * ROWS * HIDDEN * DETER
+
+
+def k_onto_partitions(nc, banks, ident_f32, rows, grouped):
+    words = rows.bitcast(F32).rearrange("p (b w j) -> p b j w", b=TILES, j=2)
+    grouped_words = grouped.bitcast(F32).rearrange("p (c j) -> p c j", j=2)
+    for half in range(2):
+        bank = banks.tile([P, 2, 2 * P], F32, tag="kT")
+        for b in range(2):
+            for j in range(2):
+                nc.tensor.transpose(bank[:, j, b * P : (b + 1) * P], words[:, 2 * half + b, j, :], ident_f32)
+        nc.scalar.copy(
+            out=grouped_words[:, half * 2 * P : (half + 1) * 2 * P, :],
+            in_=bank[:].rearrange("p j c -> p c j"),
+        )
+
+
+def tile_mamba2backbone_pa_t_kernel(tc, stoch, action, tok_w1, tok_b1, tok_nw, tok_w2, tok_b2, out):
+    nc = tc.nc
+    with ExitStack() as ctx:
+        consts = ctx.enter_context(tc.tile_pool(name="consts", bufs=1))
+        inputs = ctx.enter_context(tc.tile_pool(name="inputs", bufs=GROUPS))
+        packed = ctx.enter_context(tc.tile_pool(name="packed", bufs=3))
+        hidden_pool = ctx.enter_context(tc.tile_pool(name="hidden", bufs=3 * TILES))
+        scratch = ctx.enter_context(tc.tile_pool(name="scratch", bufs=4))
+        kT_banks = ctx.enter_context(tc.psum_pool(name="kT_banks", bufs=2))
+        h_banks = ctx.enter_context(tc.psum_pool(name="h_banks", bufs=3))
+        zT_banks = ctx.enter_context(tc.psum_pool(name="zT_banks", bufs=2))
+        o_banks = ctx.enter_context(tc.psum_pool(name="o_banks", bufs=1))
+
+        w1_rows = consts.tile([P, TILES * K1], BF16)
+        nc.sync.dma_start(
+            out=w1_rows[:].rearrange("f (b k) -> f b k", b=TILES),
+            in_=tok_w1.rearrange("(b f) k -> f b k", f=P),
+        )
+        w2_rows = consts.tile([P, HIDDEN], BF16)
+        u_rows = {}
+        for g in range(GROUPS):
+            u_rows[g] = inputs.tile([P, TILES * K1], BF16, name="u_rows")
+            u_view = u_rows[g][:].rearrange("p (i k) -> p i k", i=TILES)
+            group_rows = slice(g * GROUP, (g + 1) * GROUP)
+            nc.sync.dma_start(out=u_view[:, :, 0:STOCH], in_=stoch[group_rows, :].rearrange("(p i) k -> p i k", i=TILES))
+            nc.sync.dma_start(out=u_view[:, :, STOCH:K1], in_=action[group_rows, :].rearrange("(p i) k -> p i k", i=TILES))
+            if g == 0:
+                nc.sync.dma_start(out=w2_rows[:], in_=tok_w2)
+        b1_rows = consts.tile([P, HIDDEN], BF16)
+        nw_rows = consts.tile([P, HIDDEN], BF16)
+        b2_rows = consts.tile([P, DETER], BF16)
+        nc.scalar.dma_start(out=b1_rows[:], in_=tok_b1.partition_broadcast(P))
+        nc.scalar.dma_start(out=nw_rows[:], in_=tok_nw.partition_broadcast(P))
+        nc.scalar.dma_start(out=b2_rows[:], in_=tok_b2.partition_broadcast(P))
+
+        ident_f32 = consts.tile([P, P], F32)
+        make_identity(nc, ident_f32[:])
+        ident_bf16 = consts.tile([P, P], BF16)
+        make_identity(nc, ident_bf16[:])
+        minus_half = consts.tile([P, TILES], F32)
+        nc.vector.memset(minus_half[:], -0.5)
+        warm_in = consts.tile([P, 1], F32)
+        warm_out = consts.tile([P, 1], F32)
+        nc.vector.memset(warm_in[:], 0.0)
+        nc.scalar.activation(out=warm_out[:], in_=warm_in[:], func=ACT.Silu)
+
+        w1_grouped = consts.tile([P, HIDDEN * PACK], BF16, align_bytes=64)
+        w1_codes = consts.tile([P, HIDDEN], U32, align_bytes=64)
+        w1_scales = consts.tile([P, HIDDEN], U8, align_bytes=64)
+        k_onto_partitions(nc, kT_banks, ident_f32[:], w1_rows[:], w1_grouped[:])
+        nc.vector.quantize_mx(out=w1_codes[:].bitcast(FP8X4), scales=w1_scales[:], in_=w1_grouped[:])
+
+        w2T = zT_banks.tile([P, PACK, DETER], BF16, tag="zT")
+        for t in range(PACK):
+            nc.tensor.transpose(w2T[:, t, :], w2_rows[:, t * P : (t + 1) * P], ident_bf16[:])
+        w2_grouped = consts.tile([P, DETER * PACK], BF16, align_bytes=64)
+        w2_codes = consts.tile([P, DETER], U32, align_bytes=64)
+        w2_scales = consts.tile([P, DETER], U8, align_bytes=64)
+        nc.vector.tensor_copy(
+            out=w2_grouped[:].rearrange("q (d t) -> q d t", t=PACK), in_=w2T[:].rearrange("q t d -> q d t")
+        )
+        nc.vector.quantize_mx(out=w2_codes[:].bitcast(FP8X4), scales=w2_scales[:], in_=w2_grouped[:])
+
+        u_codes, u_scales, hb, rstd, g_grouped = {}, {}, {}, {}, {}
+
+        def pack_u(g):
+            an = u_rows[g][:].rearrange("p (i k) -> p i k", i=TILES)[:, :, STOCH:K1]
+            nc.gpsimd.tensor_scalar(out=an, in0=an, scalar1=1.0, scalar2=-1.0, op0=ALU.min, op1=ALU.max)
+            u_grouped = packed.tile([P, GROUP * PACK], BF16, align_bytes=64)
+            k_onto_partitions(nc, kT_banks, ident_f32[:], u_rows[g][:], u_grouped[:])
+            u_codes[g] = packed.tile([P, GROUP], U32, align_bytes=64, name="u_codes")
+            u_scales[g] = packed.tile([P, GROUP], U8, align_bytes=64, name="u_scales")
+            nc.vector.quantize_mx(out=u_codes[g][:].bitcast(FP8X4), scales=u_scales[g][:], in_=u_grouped[:])
+
+        def hidden(g):
+            mean_sq = scratch.tile([P, TILES], F32)
+            for i in range(TILES):
+                cols = slice(i * P, (i + 1) * P)
+                h = h_banks.tile([P, HIDDEN], F32)
+                nc.tensor.matmul_mx(
+                    out=h[:],
+                    lhsT=u_codes[g][:, cols].bitcast(FP8X4),
+                    lhsT_scale=u_scales[g][:, cols],
+                    rhs=w1_codes[:].bitcast(FP8X4),
+                    rhs_scale=w1_scales[:],
+                    start=True,
+                    stop=True,
+                )
+                hb[g, i] = hidden_pool.tile([P, HIDDEN], F32, name="hb")
+                nc.vector.tensor_tensor(out=hb[g, i][:], in0=h[:], in1=b1_rows[:], op=ALU.add)
+                squares = scratch.tile([P, HIDDEN], BF16)
+                nc.scalar.activation(
+                    out=squares[:],
+                    in_=hb[g, i][:],
+                    func=ACT.Square,
+                    scale=1.0 / math.sqrt(HIDDEN),
+                    accum_out=mean_sq[:, i : i + 1],
+                )
+            shifted = scratch.tile([P, TILES], F32)
+            nc.gpsimd.tensor_scalar(out=shifted[:], in0=mean_sq[:], scalar1=EPS, scalar2=1.0, op0=ALU.add, op1=ALU.mult)
+            rstd[g] = scratch.tile([P, TILES], F32, name="rstd")
+            nc.gpsimd.tensor_tensor(out=rstd[g][:], in0=shifted[:], in1=minus_half[:], op=ALU.pow)
+
+        def gate(g):
+            g_grouped[g] = packed.tile([P, GROUP * PACK], BF16, align_bytes=64, name="g_grouped")
+            g_view = g_grouped[g][:].rearrange("q (r t) -> q r t", t=PACK)
+            for i in range(TILES):
+                z = scratch.tile([P, HIDDEN], F32)
+                nc.vector.scalar_tensor_tensor(
+                    out=z[:], in0=hb[g, i][:], scalar=rstd[g][:, i : i + 1], in1=nw_rows[:], op0=ALU.mult, op1=ALU.mult
+                )
+                zT = zT_banks.tile([P, PACK, P], F32, tag="zT")
+                for t in range(PACK):
+                    nc.tensor.transpose(zT[:, t, :], z[:, t * P : (t + 1) * P], ident_f32[:])
+                nc.scalar.activation(
+                    out=g_view[:, i * P : (i + 1) * P, :], in_=zT[:].rearrange("q t r -> q r t"), func=ACT.Silu
+                )
+
+        def project(g):
+            g_codes = packed.tile([P, GROUP], U32, align_bytes=64)
+            g_scales = packed.tile([P, GROUP], U8, align_bytes=64)
+            nc.vector.quantize_mx(out=g_codes[:].bitcast(FP8X4), scales=g_scales[:], in_=g_grouped[g][:])
+            o = o_banks.tile([P, TILES, DETER], F32)
+            for i in range(TILES):
+                cols = slice(i * P, (i + 1) * P)
+                nc.tensor.matmul_mx(
+                    out=o[:, i, :],
+                    lhsT=g_codes[:, cols].bitcast(FP8X4),
+                    lhsT_scale=g_scales[:, cols],
+                    rhs=w2_codes[:].bitcast(FP8X4),
+                    rhs_scale=w2_scales[:],
+                    start=True,
+                    stop=True,
+                )
+            o_rows = packed.tile([P, TILES, DETER], F32)
+            nc.vector.tensor_tensor(
+                out=o_rows[:], in0=o[:], in1=b2_rows[:].unsqueeze(1).to_broadcast([P, TILES, DETER]), op=ALU.add
+            )
+            nc.sync.dma_start(
+                out=out[g * GROUP : (g + 1) * GROUP, :].rearrange("(p i) d -> p i d", i=TILES), in_=o_rows[:]
+            )
+
+        pipeline = (pack_u, hidden, gate, project)
+        for step in range(GROUPS + len(pipeline) - 1):
+            for lag in reversed(range(len(pipeline))):
+                g = step - lag
+                if 0 <= g < GROUPS:
+                    pipeline[lag](g)

@@ -20,52 +20,61 @@ EPS = 1e-4
 TILES = 4
 GROUP = TILES * P
 GROUPS = ROWS // GROUP
+N_TILES = ROWS // P
+
+LOAD_LEAD = 16
+CLAMP_LEAD = 7
+TRANSPOSE_U_LEAD = 5
+EVACUATE_U_LEAD = 4
+QUANTISE_U_LEAD = 2
+MATMUL_1_LEAD = 1
+PAIR = 2
+NORMALISE_LAG = 4
+SILU_LAG = NORMALISE_LAG + 1
+QUANTISE_G_LAG = SILU_LAG + TILES
+MATMUL_2_LAG = QUANTISE_G_LAG + 1
+STORE_LAG = MATMUL_2_LAG + 2
 
 FLOPS = 2 * ROWS * K1 * HIDDEN + 2 * ROWS * HIDDEN * DETER
 
 
-def k_onto_partitions(nc, banks, ident_f32, rows, grouped):
+def transpose_words(nc, banks, ident_f32, rows, half):
     words = rows.bitcast(F32).rearrange("p (b w j) -> p b j w", b=TILES, j=2)
-    grouped_words = grouped.bitcast(F32).rearrange("p (c j) -> p c j", j=2)
-    for half in range(2):
-        bank = banks.tile([P, 2, 2 * P], F32, tag="kT")
-        for b in range(2):
-            for j in range(2):
-                nc.tensor.transpose(bank[:, j, b * P : (b + 1) * P], words[:, 2 * half + b, j, :], ident_f32)
-        nc.scalar.copy(
-            out=grouped_words[:, half * 2 * P : (half + 1) * 2 * P, :],
-            in_=bank[:].rearrange("p j c -> p c j"),
-        )
+    bank = banks.tile([P, 2, 2 * P], F32, tag="kT")
+    for b in range(2):
+        for j in range(2):
+            nc.tensor.transpose(bank[:, j, b * P : (b + 1) * P], words[:, 2 * half + b, j, :], ident_f32)
+    return bank
+
+
+def interleave_words(nc, bank, grouped, half):
+    grouped_words = grouped.bitcast(F32).rearrange("q (c j) -> q c j", j=2)
+    nc.scalar.copy(
+        out=grouped_words[:, half * 2 * P : (half + 1) * 2 * P, :], in_=bank[:].rearrange("q j c -> q c j")
+    )
 
 
 def tile_mamba2backbone_pa_t_kernel(tc, stoch, action, tok_w1, tok_b1, tok_nw, tok_w2, tok_b2, out):
     nc = tc.nc
     with ExitStack() as ctx:
         consts = ctx.enter_context(tc.tile_pool(name="consts", bufs=1))
-        inputs = ctx.enter_context(tc.tile_pool(name="inputs", bufs=GROUPS))
+        inputs = ctx.enter_context(tc.tile_pool(name="inputs", bufs=5))
         packed = ctx.enter_context(tc.tile_pool(name="packed", bufs=3))
-        hidden_pool = ctx.enter_context(tc.tile_pool(name="hidden", bufs=3 * TILES))
-        scratch = ctx.enter_context(tc.tile_pool(name="scratch", bufs=4))
+        hidden_pool = ctx.enter_context(tc.tile_pool(name="hidden", bufs=NORMALISE_LAG + 3))
+        scratch = ctx.enter_context(tc.tile_pool(name="scratch", bufs=3))
+        columns = ctx.enter_context(tc.tile_pool(name="columns", bufs=NORMALISE_LAG + 5))
         kT_banks = ctx.enter_context(tc.psum_pool(name="kT_banks", bufs=2))
-        h_banks = ctx.enter_context(tc.psum_pool(name="h_banks", bufs=3))
-        zT_banks = ctx.enter_context(tc.psum_pool(name="zT_banks", bufs=2))
+        h_banks = ctx.enter_context(tc.psum_pool(name="h_banks", bufs=2))
+        zT_banks = ctx.enter_context(tc.psum_pool(name="zT_banks", bufs=3))
         o_banks = ctx.enter_context(tc.psum_pool(name="o_banks", bufs=1))
+        ctx.enter_context(tc.manual_schedule())
 
         w1_rows = consts.tile([P, TILES * K1], BF16)
         nc.sync.dma_start(
-            out=w1_rows[:].rearrange("f (b k) -> f b k", b=TILES),
-            in_=tok_w1.rearrange("(b f) k -> f b k", f=P),
+            out=w1_rows[:].rearrange("f (b k) -> f b k", b=TILES), in_=tok_w1.rearrange("(b f) k -> f b k", f=P)
         )
         w2_rows = consts.tile([P, HIDDEN], BF16)
-        u_rows = {}
-        for g in range(GROUPS):
-            u_rows[g] = inputs.tile([P, TILES * K1], BF16, name="u_rows")
-            u_view = u_rows[g][:].rearrange("p (i k) -> p i k", i=TILES)
-            group_rows = slice(g * GROUP, (g + 1) * GROUP)
-            nc.sync.dma_start(out=u_view[:, :, 0:STOCH], in_=stoch[group_rows, :].rearrange("(p i) k -> p i k", i=TILES))
-            nc.sync.dma_start(out=u_view[:, :, STOCH:K1], in_=action[group_rows, :].rearrange("(p i) k -> p i k", i=TILES))
-            if g == 0:
-                nc.sync.dma_start(out=w2_rows[:], in_=tok_w2)
+        nc.scalar.dma_start(out=w2_rows[:], in_=tok_w2)
         b1_rows = consts.tile([P, HIDDEN], BF16)
         nw_rows = consts.tile([P, HIDDEN], BF16)
         b2_rows = consts.tile([P, DETER], BF16)
@@ -77,7 +86,7 @@ def tile_mamba2backbone_pa_t_kernel(tc, stoch, action, tok_w1, tok_b1, tok_nw, t
         make_identity(nc, ident_f32[:])
         ident_bf16 = consts.tile([P, P], BF16)
         make_identity(nc, ident_bf16[:])
-        minus_half = consts.tile([P, TILES], F32)
+        minus_half = consts.tile([P, PAIR], F32)
         nc.vector.memset(minus_half[:], -0.5)
         warm_in = consts.tile([P, 1], F32)
         warm_out = consts.tile([P, 1], F32)
@@ -87,7 +96,9 @@ def tile_mamba2backbone_pa_t_kernel(tc, stoch, action, tok_w1, tok_b1, tok_nw, t
         w1_grouped = consts.tile([P, HIDDEN * PACK], BF16, align_bytes=64)
         w1_codes = consts.tile([P, HIDDEN], U32, align_bytes=64)
         w1_scales = consts.tile([P, HIDDEN], U8, align_bytes=64)
-        k_onto_partitions(nc, kT_banks, ident_f32[:], w1_rows[:], w1_grouped[:])
+        for half in range(2):
+            w1_bank = transpose_words(nc, kT_banks, ident_f32[:], w1_rows[:], half)
+            interleave_words(nc, w1_bank, w1_grouped[:], half)
         nc.vector.quantize_mx(out=w1_codes[:].bitcast(FP8X4), scales=w1_scales[:], in_=w1_grouped[:])
 
         w2T = zT_banks.tile([P, PACK, DETER], BF16, tag="zT")
@@ -101,88 +112,136 @@ def tile_mamba2backbone_pa_t_kernel(tc, stoch, action, tok_w1, tok_b1, tok_nw, t
         )
         nc.vector.quantize_mx(out=w2_codes[:].bitcast(FP8X4), scales=w2_scales[:], in_=w2_grouped[:])
 
-        u_codes, u_scales, hb, rstd, g_grouped = {}, {}, {}, {}, {}
+        u_rows, u_banks, u_grouped, u_codes, u_scales = {}, {}, {}, {}, {}
+        h, hb, mean_sq, rstd, zT, g_grouped, g_codes, g_scales, o = {}, {}, {}, {}, {}, {}, {}, {}, {}
 
-        def pack_u(g):
+        def load_u(g):
+            u_rows[g] = inputs.tile([P, TILES * K1], BF16, name="u_rows")
+            u_view = u_rows[g][:].rearrange("p (i k) -> p i k", i=TILES)
+            rows = slice(g * GROUP, (g + 1) * GROUP)
+            nc.sync.dma_start(out=u_view[:, :, 0:STOCH], in_=stoch[rows, :].rearrange("(p i) k -> p i k", i=TILES))
+            nc.sync.dma_start(out=u_view[:, :, STOCH:K1], in_=action[rows, :].rearrange("(p i) k -> p i k", i=TILES))
+
+        def clamp_action(g):
             an = u_rows[g][:].rearrange("p (i k) -> p i k", i=TILES)[:, :, STOCH:K1]
             nc.gpsimd.tensor_scalar(out=an, in0=an, scalar1=1.0, scalar2=-1.0, op0=ALU.min, op1=ALU.max)
-            u_grouped = packed.tile([P, GROUP * PACK], BF16, align_bytes=64)
-            k_onto_partitions(nc, kT_banks, ident_f32[:], u_rows[g][:], u_grouped[:])
+
+        def transpose_u(g, half):
+            u_banks[g, half] = transpose_words(nc, kT_banks, ident_f32[:], u_rows[g][:], half)
+
+        def evacuate_u(g, half):
+            if half == 0:
+                u_grouped[g] = packed.tile([P, GROUP * PACK], BF16, align_bytes=64, name="u_grouped")
+            interleave_words(nc, u_banks[g, half], u_grouped[g][:], half)
+
+        def quantise_u(g):
             u_codes[g] = packed.tile([P, GROUP], U32, align_bytes=64, name="u_codes")
             u_scales[g] = packed.tile([P, GROUP], U8, align_bytes=64, name="u_scales")
-            nc.vector.quantize_mx(out=u_codes[g][:].bitcast(FP8X4), scales=u_scales[g][:], in_=u_grouped[:])
+            nc.vector.quantize_mx(out=u_codes[g][:].bitcast(FP8X4), scales=u_scales[g][:], in_=u_grouped[g][:])
 
-        def hidden(g):
-            mean_sq = scratch.tile([P, TILES], F32)
-            for i in range(TILES):
-                cols = slice(i * P, (i + 1) * P)
-                h = h_banks.tile([P, HIDDEN], F32)
-                nc.tensor.matmul_mx(
-                    out=h[:],
-                    lhsT=u_codes[g][:, cols].bitcast(FP8X4),
-                    lhsT_scale=u_scales[g][:, cols],
-                    rhs=w1_codes[:].bitcast(FP8X4),
-                    rhs_scale=w1_scales[:],
-                    start=True,
-                    stop=True,
-                )
-                hb[g, i] = hidden_pool.tile([P, HIDDEN], F32, name="hb")
-                nc.vector.tensor_tensor(out=hb[g, i][:], in0=h[:], in1=b1_rows[:], op=ALU.add)
-                squares = scratch.tile([P, HIDDEN], BF16)
-                nc.scalar.activation(
-                    out=squares[:],
-                    in_=hb[g, i][:],
-                    func=ACT.Square,
-                    scale=1.0 / math.sqrt(HIDDEN),
-                    accum_out=mean_sq[:, i : i + 1],
-                )
-            shifted = scratch.tile([P, TILES], F32)
-            nc.gpsimd.tensor_scalar(out=shifted[:], in0=mean_sq[:], scalar1=EPS, scalar2=1.0, op0=ALU.add, op1=ALU.mult)
-            rstd[g] = scratch.tile([P, TILES], F32, name="rstd")
-            nc.gpsimd.tensor_tensor(out=rstd[g][:], in0=shifted[:], in1=minus_half[:], op=ALU.pow)
+        def first_matmul(n):
+            g, i = divmod(n, TILES)
+            cols = slice(i * P, (i + 1) * P)
+            h[n] = h_banks.tile([P, HIDDEN], F32, name="h")
+            nc.tensor.matmul_mx(
+                out=h[n][:],
+                lhsT=u_codes[g][:, cols].bitcast(FP8X4),
+                lhsT_scale=u_scales[g][:, cols],
+                rhs=w1_codes[:].bitcast(FP8X4),
+                rhs_scale=w1_scales[:],
+                start=True,
+                stop=True,
+            )
 
-        def gate(g):
-            g_grouped[g] = packed.tile([P, GROUP * PACK], BF16, align_bytes=64, name="g_grouped")
+        def add_bias(n):
+            hb[n] = hidden_pool.tile([P, HIDDEN], F32, name="hb")
+            nc.vector.tensor_tensor(out=hb[n][:], in0=h[n][:], in1=b1_rows[:], op=ALU.add)
+            squares = scratch.tile([P, HIDDEN], BF16)
+            pair, j = divmod(n, PAIR)
+            if j == 0:
+                mean_sq[pair] = columns.tile([P, PAIR], F32, name="mean_sq")
+            nc.scalar.activation(
+                out=squares[:],
+                in_=hb[n][:],
+                func=ACT.Square,
+                scale=1.0 / math.sqrt(HIDDEN),
+                accum_out=mean_sq[pair][:, j : j + 1],
+            )
+            if j == PAIR - 1:
+                shifted = columns.tile([P, PAIR], F32)
+                nc.gpsimd.tensor_scalar(
+                    out=shifted[:], in0=mean_sq[pair][:], scalar1=EPS, scalar2=1.0, op0=ALU.add, op1=ALU.mult
+                )
+                rstd[pair] = columns.tile([P, PAIR], F32, name="rstd")
+                nc.gpsimd.tensor_tensor(out=rstd[pair][:], in0=shifted[:], in1=minus_half[:], op=ALU.pow)
+
+        def normalise(n):
+            z = scratch.tile([P, HIDDEN], F32)
+            pair, j = divmod(n, PAIR)
+            nc.vector.scalar_tensor_tensor(
+                out=z[:], in0=hb[n][:], scalar=rstd[pair][:, j : j + 1], in1=nw_rows[:], op0=ALU.mult, op1=ALU.mult
+            )
+            zT[n] = zT_banks.tile([P, PACK, P], F32, tag="zT", name="zT")
+            for t in range(PACK):
+                nc.tensor.transpose(zT[n][:, t, :], z[:, t * P : (t + 1) * P], ident_f32[:])
+
+        def silu(n):
+            g, i = divmod(n, TILES)
+            if i == 0:
+                g_grouped[g] = packed.tile([P, GROUP * PACK], BF16, align_bytes=64, name="g_grouped")
             g_view = g_grouped[g][:].rearrange("q (r t) -> q r t", t=PACK)
-            for i in range(TILES):
-                z = scratch.tile([P, HIDDEN], F32)
-                nc.vector.scalar_tensor_tensor(
-                    out=z[:], in0=hb[g, i][:], scalar=rstd[g][:, i : i + 1], in1=nw_rows[:], op0=ALU.mult, op1=ALU.mult
-                )
-                zT = zT_banks.tile([P, PACK, P], F32, tag="zT")
-                for t in range(PACK):
-                    nc.tensor.transpose(zT[:, t, :], z[:, t * P : (t + 1) * P], ident_f32[:])
-                nc.scalar.activation(
-                    out=g_view[:, i * P : (i + 1) * P, :], in_=zT[:].rearrange("q t r -> q r t"), func=ACT.Silu
-                )
+            nc.scalar.activation(
+                out=g_view[:, i * P : (i + 1) * P, :], in_=zT[n][:].rearrange("q t r -> q r t"), func=ACT.Silu
+            )
 
-        def project(g):
-            g_codes = packed.tile([P, GROUP], U32, align_bytes=64)
-            g_scales = packed.tile([P, GROUP], U8, align_bytes=64)
-            nc.vector.quantize_mx(out=g_codes[:].bitcast(FP8X4), scales=g_scales[:], in_=g_grouped[g][:])
-            o = o_banks.tile([P, TILES, DETER], F32)
+        def quantise_g(g):
+            g_codes[g] = packed.tile([P, GROUP], U32, align_bytes=64, name="g_codes")
+            g_scales[g] = packed.tile([P, GROUP], U8, align_bytes=64, name="g_scales")
+            nc.vector.quantize_mx(out=g_codes[g][:].bitcast(FP8X4), scales=g_scales[g][:], in_=g_grouped[g][:])
+
+        def second_matmul(g):
+            o[g] = o_banks.tile([P, TILES, DETER], F32, name="o")
             for i in range(TILES):
                 cols = slice(i * P, (i + 1) * P)
                 nc.tensor.matmul_mx(
-                    out=o[:, i, :],
-                    lhsT=g_codes[:, cols].bitcast(FP8X4),
-                    lhsT_scale=g_scales[:, cols],
+                    out=o[g][:, i, :],
+                    lhsT=g_codes[g][:, cols].bitcast(FP8X4),
+                    lhsT_scale=g_scales[g][:, cols],
                     rhs=w2_codes[:].bitcast(FP8X4),
                     rhs_scale=w2_scales[:],
                     start=True,
                     stop=True,
                 )
+
+        def store(g):
             o_rows = packed.tile([P, TILES, DETER], F32)
             nc.vector.tensor_tensor(
-                out=o_rows[:], in0=o[:], in1=b2_rows[:].unsqueeze(1).to_broadcast([P, TILES, DETER]), op=ALU.add
+                out=o_rows[:], in0=o[g][:], in1=b2_rows[:].unsqueeze(1).to_broadcast([P, TILES, DETER]), op=ALU.add
             )
             nc.sync.dma_start(
                 out=out[g * GROUP : (g + 1) * GROUP, :].rearrange("(p i) d -> p i d", i=TILES), in_=o_rows[:]
             )
 
-        pipeline = (pack_u, hidden, gate, project)
-        for step in range(GROUPS + len(pipeline) - 1):
-            for lag in reversed(range(len(pipeline))):
-                g = step - lag
-                if 0 <= g < GROUPS:
-                    pipeline[lag](g)
+        def for_tile(work, n):
+            if 0 <= n < N_TILES:
+                work(n)
+
+        def for_group(work, n, *half):
+            if 0 <= n < N_TILES and n % TILES == 0:
+                work(n // TILES, *half)
+
+        for n in range(-LOAD_LEAD, N_TILES + STORE_LAG):
+            for_group(load_u, n + LOAD_LEAD)
+            for_group(clamp_action, n + CLAMP_LEAD)
+            for_tile(first_matmul, n + MATMUL_1_LEAD)
+            for_group(second_matmul, n - MATMUL_2_LAG)
+            for_group(transpose_u, n + TRANSPOSE_U_LEAD, 0)
+            for_group(transpose_u, n + TRANSPOSE_U_LEAD - 1, 1)
+            for_group(evacuate_u, n + EVACUATE_U_LEAD, 0)
+            for_group(evacuate_u, n + EVACUATE_U_LEAD - 1, 1)
+            for_tile(silu, n - SILU_LAG)
+            for_tile(add_bias, n)
+            for_tile(normalise, n - NORMALISE_LAG)
+            for_group(quantise_u, n + QUANTISE_U_LEAD)
+            for_group(quantise_g, n - QUANTISE_G_LAG)
+            for_group(store, n - STORE_LAG)

@@ -17,62 +17,58 @@ PACK = 4
 ROWS, STOCH, ACTION, HIDDEN, DETER = 8192, 384, 128, 512, 128
 K1 = STOCH + ACTION
 EPS = 1e-4
-TILES = 4
+TILES = 2
 GROUP = TILES * P
 GROUPS = ROWS // GROUP
-N_TILES = ROWS // P
-
-LOAD_LEAD = 16
-CLAMP_LEAD = 7
-TRANSPOSE_U_LEAD = 5
-EVACUATE_U_LEAD = 4
-QUANTISE_U_LEAD = 2
-MATMUL_1_LEAD = 1
-PAIR = 2
-NORMALISE_LAG = 4
-SILU_LAG = NORMALISE_LAG + 1
-QUANTISE_G_LAG = SILU_LAG + TILES
-MATMUL_2_LAG = QUANTISE_G_LAG + 1
-STORE_LAG = MATMUL_2_LAG + 2
 
 FLOPS = 2 * ROWS * K1 * HIDDEN + 2 * ROWS * HIDDEN * DETER
 
+LOAD_LEAD = 8
+CLAMP_LEAD = 4
+TRANSPOSE_U_LEAD = 3
+EVACUATE_U_LEAD = 2
+QUANTISE_U_LEAD = 2
+MATMUL_1_LEAD = 1
+NORMALISE_LAG = 2
+SILU_LAG = NORMALISE_LAG + 1
+QUANTISE_G_LAG = SILU_LAG + 1
+MATMUL_2_LAG = QUANTISE_G_LAG + 1
+STORE_LAG = MATMUL_2_LAG + 1
 
-def transpose_words(nc, banks, ident_f32, rows, half):
+
+def transpose_words(nc, banks, ident_f32, rows):
     words = rows.bitcast(F32).rearrange("p (b w j) -> p b j w", b=TILES, j=2)
-    bank = banks.tile([P, 2, 2 * P], F32, tag="kT")
-    for b in range(2):
+    bank = banks.tile([P, 2, TILES * P], F32, tag="kT")
+    for b in range(TILES):
         for j in range(2):
-            nc.tensor.transpose(bank[:, j, b * P : (b + 1) * P], words[:, 2 * half + b, j, :], ident_f32)
+            nc.tensor.transpose(bank[:, j, b * P : (b + 1) * P], words[:, b, j, :], ident_f32)
     return bank
 
 
-def interleave_words(nc, bank, grouped, half):
-    grouped_words = grouped.bitcast(F32).rearrange("q (c j) -> q c j", j=2)
-    nc.scalar.copy(
-        out=grouped_words[:, half * 2 * P : (half + 1) * 2 * P, :], in_=bank[:].rearrange("q j c -> q c j")
-    )
+def interleave_words(nc, bank, grouped_words):
+    nc.scalar.copy(out=grouped_words.rearrange("q (c j) -> q c j", j=2), in_=bank[:].rearrange("q j c -> q c j"))
 
 
 def tile_mamba2backbone_pa_t_kernel(tc, stoch, action, tok_w1, tok_b1, tok_nw, tok_w2, tok_b2, out):
     nc = tc.nc
     with ExitStack() as ctx:
         consts = ctx.enter_context(tc.tile_pool(name="consts", bufs=1))
-        inputs = ctx.enter_context(tc.tile_pool(name="inputs", bufs=5))
-        packed = ctx.enter_context(tc.tile_pool(name="packed", bufs=3))
-        hidden_pool = ctx.enter_context(tc.tile_pool(name="hidden", bufs=NORMALISE_LAG + 3))
-        scratch = ctx.enter_context(tc.tile_pool(name="scratch", bufs=3))
-        columns = ctx.enter_context(tc.tile_pool(name="columns", bufs=NORMALISE_LAG + 5))
+        inputs = ctx.enter_context(tc.tile_pool(name="inputs", bufs=LOAD_LEAD))
+        packed = ctx.enter_context(tc.tile_pool(name="packed", bufs=4))
+        hidden_pool = ctx.enter_context(tc.tile_pool(name="hidden", bufs=(NORMALISE_LAG + 2) * TILES))
+        scratch = ctx.enter_context(tc.tile_pool(name="scratch", bufs=4))
+        columns = ctx.enter_context(tc.tile_pool(name="columns", bufs=NORMALISE_LAG + 3))
         kT_banks = ctx.enter_context(tc.psum_pool(name="kT_banks", bufs=2))
-        h_banks = ctx.enter_context(tc.psum_pool(name="h_banks", bufs=2))
-        zT_banks = ctx.enter_context(tc.psum_pool(name="zT_banks", bufs=3))
-        o_banks = ctx.enter_context(tc.psum_pool(name="o_banks", bufs=1))
+        h_banks = ctx.enter_context(tc.psum_pool(name="h_banks", bufs=TILES))
+        zT_banks = ctx.enter_context(tc.psum_pool(name="zT_banks", bufs=TILES))
+        o_banks = ctx.enter_context(tc.psum_pool(name="o_banks", bufs=2))
         ctx.enter_context(tc.manual_schedule())
 
-        w1_rows = consts.tile([P, TILES * K1], BF16)
-        nc.sync.dma_start(
-            out=w1_rows[:].rearrange("f (b k) -> f b k", b=TILES), in_=tok_w1.rearrange("(b f) k -> f b k", f=P)
-        )
+        w1_blocks = tok_w1.rearrange("(a b f) k -> a f b k", b=TILES, f=P)
+        w1_rows = []
+        for a in range(HIDDEN // GROUP):
+            w1_rows.append(consts.tile([P, TILES * K1], BF16, name="w1_rows%d" % a))
+            nc.sync.dma_start(out=w1_rows[a][:].rearrange("f (b k) -> f b k", b=TILES), in_=w1_blocks[a])
         w2_rows = consts.tile([P, HIDDEN], BF16)
         nc.scalar.dma_start(out=w2_rows[:], in_=tok_w2)
         b1_rows = consts.tile([P, HIDDEN], BF16)
@@ -86,7 +82,7 @@ def tile_mamba2backbone_pa_t_kernel(tc, stoch, action, tok_w1, tok_b1, tok_nw, t
         make_identity(nc, ident_f32[:])
         ident_bf16 = consts.tile([P, P], BF16)
         make_identity(nc, ident_bf16[:])
-        minus_half = consts.tile([P, PAIR], F32)
+        minus_half = consts.tile([P, TILES], F32)
         nc.vector.memset(minus_half[:], -0.5)
         warm_in = consts.tile([P, 1], F32)
         warm_out = consts.tile([P, 1], F32)
@@ -96,9 +92,9 @@ def tile_mamba2backbone_pa_t_kernel(tc, stoch, action, tok_w1, tok_b1, tok_nw, t
         w1_grouped = consts.tile([P, HIDDEN * PACK], BF16, align_bytes=64)
         w1_codes = consts.tile([P, HIDDEN], U32, align_bytes=64)
         w1_scales = consts.tile([P, HIDDEN], U8, align_bytes=64)
-        for half in range(2):
-            w1_bank = transpose_words(nc, kT_banks, ident_f32[:], w1_rows[:], half)
-            interleave_words(nc, w1_bank, w1_grouped[:], half)
+        for a in range(HIDDEN // GROUP):
+            w1_bank = transpose_words(nc, kT_banks, ident_f32[:], w1_rows[a][:])
+            interleave_words(nc, w1_bank, w1_grouped[:].bitcast(F32)[:, a * GROUP * 2 : (a + 1) * GROUP * 2])
         nc.vector.quantize_mx(out=w1_codes[:].bitcast(FP8X4), scales=w1_scales[:], in_=w1_grouped[:])
 
         w2T = zT_banks.tile([P, PACK, DETER], BF16, tag="zT")
@@ -112,8 +108,8 @@ def tile_mamba2backbone_pa_t_kernel(tc, stoch, action, tok_w1, tok_b1, tok_nw, t
         )
         nc.vector.quantize_mx(out=w2_codes[:].bitcast(FP8X4), scales=w2_scales[:], in_=w2_grouped[:])
 
-        u_rows, u_banks, u_grouped, u_codes, u_scales = {}, {}, {}, {}, {}
-        h, hb, mean_sq, rstd, zT, g_grouped, g_codes, g_scales, o = {}, {}, {}, {}, {}, {}, {}, {}, {}
+        u_rows, u_bank, u_grouped, u_codes, u_scales = {}, {}, {}, {}, {}
+        h, hb, rstd, zT, g_grouped, g_codes, g_scales, o = {}, {}, {}, {}, {}, {}, {}, {}
 
         def load_u(g):
             u_rows[g] = inputs.tile([P, TILES * K1], BF16, name="u_rows")
@@ -126,73 +122,68 @@ def tile_mamba2backbone_pa_t_kernel(tc, stoch, action, tok_w1, tok_b1, tok_nw, t
             an = u_rows[g][:].rearrange("p (i k) -> p i k", i=TILES)[:, :, STOCH:K1]
             nc.gpsimd.tensor_scalar(out=an, in0=an, scalar1=1.0, scalar2=-1.0, op0=ALU.min, op1=ALU.max)
 
-        def transpose_u(g, half):
-            u_banks[g, half] = transpose_words(nc, kT_banks, ident_f32[:], u_rows[g][:], half)
+        def transpose_u(g):
+            u_bank[g] = transpose_words(nc, kT_banks, ident_f32[:], u_rows[g][:])
 
-        def evacuate_u(g, half):
-            if half == 0:
-                u_grouped[g] = packed.tile([P, GROUP * PACK], BF16, align_bytes=64, name="u_grouped")
-            interleave_words(nc, u_banks[g, half], u_grouped[g][:], half)
+        def evacuate_u(g):
+            u_grouped[g] = packed.tile([P, GROUP * PACK], BF16, align_bytes=64, name="u_grouped")
+            interleave_words(nc, u_bank[g], u_grouped[g][:].bitcast(F32))
 
         def quantise_u(g):
             u_codes[g] = packed.tile([P, GROUP], U32, align_bytes=64, name="u_codes")
             u_scales[g] = packed.tile([P, GROUP], U8, align_bytes=64, name="u_scales")
             nc.vector.quantize_mx(out=u_codes[g][:].bitcast(FP8X4), scales=u_scales[g][:], in_=u_grouped[g][:])
 
-        def first_matmul(n):
-            g, i = divmod(n, TILES)
-            cols = slice(i * P, (i + 1) * P)
-            h[n] = h_banks.tile([P, HIDDEN], F32, name="h")
-            nc.tensor.matmul_mx(
-                out=h[n][:],
-                lhsT=u_codes[g][:, cols].bitcast(FP8X4),
-                lhsT_scale=u_scales[g][:, cols],
-                rhs=w1_codes[:].bitcast(FP8X4),
-                rhs_scale=w1_scales[:],
-                start=True,
-                stop=True,
-            )
-
-        def add_bias(n):
-            hb[n] = hidden_pool.tile([P, HIDDEN], F32, name="hb")
-            nc.vector.tensor_tensor(out=hb[n][:], in0=h[n][:], in1=b1_rows[:], op=ALU.add)
-            squares = scratch.tile([P, HIDDEN], BF16)
-            pair, j = divmod(n, PAIR)
-            if j == 0:
-                mean_sq[pair] = columns.tile([P, PAIR], F32, name="mean_sq")
-            nc.scalar.activation(
-                out=squares[:],
-                in_=hb[n][:],
-                func=ACT.Square,
-                scale=1.0 / math.sqrt(HIDDEN),
-                accum_out=mean_sq[pair][:, j : j + 1],
-            )
-            if j == PAIR - 1:
-                shifted = columns.tile([P, PAIR], F32)
-                nc.gpsimd.tensor_scalar(
-                    out=shifted[:], in0=mean_sq[pair][:], scalar1=EPS, scalar2=1.0, op0=ALU.add, op1=ALU.mult
+        def first_matmul(g):
+            for i in range(TILES):
+                cols = slice(i * P, (i + 1) * P)
+                h[g, i] = h_banks.tile([P, HIDDEN], F32, name="h")
+                nc.tensor.matmul_mx(
+                    out=h[g, i][:],
+                    lhsT=u_codes[g][:, cols].bitcast(FP8X4),
+                    lhsT_scale=u_scales[g][:, cols],
+                    rhs=w1_codes[:].bitcast(FP8X4),
+                    rhs_scale=w1_scales[:],
+                    start=True,
+                    stop=True,
                 )
-                rstd[pair] = columns.tile([P, PAIR], F32, name="rstd")
-                nc.gpsimd.tensor_tensor(out=rstd[pair][:], in0=shifted[:], in1=minus_half[:], op=ALU.pow)
 
-        def normalise(n):
-            z = scratch.tile([P, HIDDEN], F32)
-            pair, j = divmod(n, PAIR)
-            nc.vector.scalar_tensor_tensor(
-                out=z[:], in0=hb[n][:], scalar=rstd[pair][:, j : j + 1], in1=nw_rows[:], op0=ALU.mult, op1=ALU.mult
-            )
-            zT[n] = zT_banks.tile([P, PACK, P], F32, tag="zT", name="zT")
-            for t in range(PACK):
-                nc.tensor.transpose(zT[n][:, t, :], z[:, t * P : (t + 1) * P], ident_f32[:])
+        def add_bias(g):
+            for i in range(TILES):
+                hb[g, i] = hidden_pool.tile([P, HIDDEN], F32, name="hb")
+                nc.vector.tensor_tensor(out=hb[g, i][:], in0=h[g, i][:], in1=b1_rows[:], op=ALU.add)
+            mean_sq = columns.tile([P, TILES], F32)
+            for i in range(TILES):
+                squares = scratch.tile([P, HIDDEN], BF16)
+                nc.scalar.activation(
+                    out=squares[:],
+                    in_=hb[g, i][:],
+                    func=ACT.Square,
+                    scale=1.0 / math.sqrt(HIDDEN),
+                    accum_out=mean_sq[:, i : i + 1],
+                )
+            shifted = columns.tile([P, TILES], F32)
+            nc.gpsimd.tensor_scalar(out=shifted[:], in0=mean_sq[:], scalar1=EPS, scalar2=1.0, op0=ALU.add, op1=ALU.mult)
+            rstd[g] = columns.tile([P, TILES], F32, name="rstd")
+            nc.gpsimd.tensor_tensor(out=rstd[g][:], in0=shifted[:], in1=minus_half[:], op=ALU.pow)
 
-        def silu(n):
-            g, i = divmod(n, TILES)
-            if i == 0:
-                g_grouped[g] = packed.tile([P, GROUP * PACK], BF16, align_bytes=64, name="g_grouped")
+        def normalise(g):
+            for i in range(TILES):
+                z = scratch.tile([P, HIDDEN], F32)
+                nc.vector.scalar_tensor_tensor(
+                    out=z[:], in0=hb[g, i][:], scalar=rstd[g][:, i : i + 1], in1=nw_rows[:], op0=ALU.mult, op1=ALU.mult
+                )
+                zT[g, i] = zT_banks.tile([P, PACK, P], F32, tag="zT", name="zT")
+                for t in range(PACK):
+                    nc.tensor.transpose(zT[g, i][:, t, :], z[:, t * P : (t + 1) * P], ident_f32[:])
+
+        def silu(g):
+            g_grouped[g] = packed.tile([P, GROUP * PACK], BF16, align_bytes=64, name="g_grouped")
             g_view = g_grouped[g][:].rearrange("q (r t) -> q r t", t=PACK)
-            nc.scalar.activation(
-                out=g_view[:, i * P : (i + 1) * P, :], in_=zT[n][:].rearrange("q t r -> q r t"), func=ACT.Silu
-            )
+            for i in range(TILES):
+                nc.scalar.activation(
+                    out=g_view[:, i * P : (i + 1) * P, :], in_=zT[g, i][:].rearrange("q t r -> q r t"), func=ACT.Silu
+                )
 
         def quantise_g(g):
             g_codes[g] = packed.tile([P, GROUP], U32, align_bytes=64, name="g_codes")
@@ -222,26 +213,20 @@ def tile_mamba2backbone_pa_t_kernel(tc, stoch, action, tok_w1, tok_b1, tok_nw, t
                 out=out[g * GROUP : (g + 1) * GROUP, :].rearrange("(p i) d -> p i d", i=TILES), in_=o_rows[:]
             )
 
-        def for_tile(work, n):
-            if 0 <= n < N_TILES:
-                work(n)
+        def when_in_range(work, g):
+            if 0 <= g < GROUPS:
+                work(g)
 
-        def for_group(work, n, *half):
-            if 0 <= n < N_TILES and n % TILES == 0:
-                work(n // TILES, *half)
-
-        for n in range(-LOAD_LEAD, N_TILES + STORE_LAG):
-            for_group(load_u, n + LOAD_LEAD)
-            for_group(clamp_action, n + CLAMP_LEAD)
-            for_tile(first_matmul, n + MATMUL_1_LEAD)
-            for_group(second_matmul, n - MATMUL_2_LAG)
-            for_group(transpose_u, n + TRANSPOSE_U_LEAD, 0)
-            for_group(transpose_u, n + TRANSPOSE_U_LEAD - 1, 1)
-            for_group(evacuate_u, n + EVACUATE_U_LEAD, 0)
-            for_group(evacuate_u, n + EVACUATE_U_LEAD - 1, 1)
-            for_tile(silu, n - SILU_LAG)
-            for_tile(add_bias, n)
-            for_tile(normalise, n - NORMALISE_LAG)
-            for_group(quantise_u, n + QUANTISE_U_LEAD)
-            for_group(quantise_g, n - QUANTISE_G_LAG)
-            for_group(store, n - STORE_LAG)
+        for s in range(-LOAD_LEAD, GROUPS + STORE_LAG):
+            when_in_range(load_u, s + LOAD_LEAD)
+            when_in_range(clamp_action, s + CLAMP_LEAD)
+            when_in_range(transpose_u, s + TRANSPOSE_U_LEAD)
+            when_in_range(evacuate_u, s + EVACUATE_U_LEAD)
+            when_in_range(silu, s - SILU_LAG)
+            when_in_range(store, s - STORE_LAG)
+            when_in_range(second_matmul, s - MATMUL_2_LAG)
+            when_in_range(add_bias, s)
+            when_in_range(first_matmul, s + MATMUL_1_LEAD)
+            when_in_range(normalise, s - NORMALISE_LAG)
+            when_in_range(quantise_u, s + QUANTISE_U_LEAD)
+            when_in_range(quantise_g, s - QUANTISE_G_LAG)

@@ -61,7 +61,8 @@ def tile_mamba2backbone_pa_t_kernel(tc, stoch, action, tok_w1, tok_b1, tok_nw, t
         kT_banks = ctx.enter_context(tc.psum_pool(name="kT_banks", bufs=2))
         h_banks = ctx.enter_context(tc.psum_pool(name="h_banks", bufs=TILES))
         zT_banks = ctx.enter_context(tc.psum_pool(name="zT_banks", bufs=TILES))
-        o_banks = ctx.enter_context(tc.psum_pool(name="o_banks", bufs=2))
+        o_banks = ctx.enter_context(tc.psum_pool(name="o_banks", bufs=1))
+        nw_banks = ctx.enter_context(tc.psum_pool(name="nw_banks", bufs=1))
         ctx.enter_context(tc.manual_schedule())
 
         w1_blocks = tok_w1.rearrange("(a b f) k -> a f b k", b=TILES, f=P)
@@ -74,8 +75,8 @@ def tile_mamba2backbone_pa_t_kernel(tc, stoch, action, tok_w1, tok_b1, tok_nw, t
         b1_rows = consts.tile([P, HIDDEN], BF16)
         nw_rows = consts.tile([P, HIDDEN], BF16)
         b2_rows = consts.tile([P, DETER], BF16)
-        nc.scalar.dma_start(out=b1_rows[:], in_=tok_b1.partition_broadcast(P))
         nc.scalar.dma_start(out=nw_rows[:], in_=tok_nw.partition_broadcast(P))
+        nc.scalar.dma_start(out=b1_rows[:], in_=tok_b1.partition_broadcast(P))
         nc.scalar.dma_start(out=b2_rows[:], in_=tok_b2.partition_broadcast(P))
 
         ident_f32 = consts.tile([P, P], F32)
@@ -107,6 +108,9 @@ def tile_mamba2backbone_pa_t_kernel(tc, stoch, action, tok_w1, tok_b1, tok_nw, t
             out=w2_grouped[:].rearrange("q (d t) -> q d t", t=PACK), in_=w2T[:].rearrange("q t d -> q d t")
         )
         nc.vector.quantize_mx(out=w2_codes[:].bitcast(FP8X4), scales=w2_scales[:], in_=w2_grouped[:])
+
+        nw_bank = nw_banks.tile([P, HIDDEN], F32)
+        nc.tensor.matmul(out=nw_bank[:], lhsT=ident_bf16[:], rhs=nw_rows[:], start=True, stop=True)
 
         u_rows, u_bank, u_grouped, u_codes, u_scales = {}, {}, {}, {}, {}
         h, hb, rstd, zT, g_grouped, g_codes, g_scales, o = {}, {}, {}, {}, {}, {}, {}, {}
@@ -171,7 +175,7 @@ def tile_mamba2backbone_pa_t_kernel(tc, stoch, action, tok_w1, tok_b1, tok_nw, t
             for i in range(TILES):
                 z = scratch.tile([P, HIDDEN], F32)
                 nc.vector.scalar_tensor_tensor(
-                    out=z[:], in0=hb[g, i][:], scalar=rstd[g][:, i : i + 1], in1=nw_rows[:], op0=ALU.mult, op1=ALU.mult
+                    out=z[:], in0=hb[g, i][:], scalar=rstd[g][:, i : i + 1], in1=nw_bank[:], op0=ALU.mult, op1=ALU.mult
                 )
                 zT[g, i] = zT_banks.tile([P, PACK, P], F32, tag="zT", name="zT")
                 for t in range(PACK):

@@ -65,6 +65,15 @@ def tile_mamba2backbone_pa_t_kernel(tc, stoch, action, tok_w1, tok_b1, tok_nw, t
         nw_banks = ctx.enter_context(tc.psum_pool(name="nw_banks", bufs=1))
         ctx.enter_context(tc.manual_schedule())
 
+        b1_row = consts.tile([P, HIDDEN], BF16)
+        nc.vector.memset(b1_row[:], 0.0)
+        nc.sync.dma_start(out=b1_row[0:1, :], in_=tok_b1.unsqueeze(0))
+        ones = consts.tile([P, P], BF16)
+        nc.vector.memset(ones[:], 1.0)
+        nw_b2_row = consts.tile([P, HIDDEN + DETER], BF16)
+        nc.vector.memset(nw_b2_row[:], 0.0)
+        nc.scalar.dma_start(out=nw_b2_row[0:1, 0:HIDDEN], in_=tok_nw.unsqueeze(0))
+        nc.scalar.dma_start(out=nw_b2_row[0:1, HIDDEN : HIDDEN + DETER], in_=tok_b2.unsqueeze(0))
         w1_blocks = tok_w1.rearrange("(a b f) k -> a f b k", b=TILES, f=P)
         w1_rows = []
         for a in range(HIDDEN // GROUP):
@@ -72,12 +81,6 @@ def tile_mamba2backbone_pa_t_kernel(tc, stoch, action, tok_w1, tok_b1, tok_nw, t
             nc.sync.dma_start(out=w1_rows[a][:].rearrange("f (b k) -> f b k", b=TILES), in_=w1_blocks[a])
         w2_rows = consts.tile([P, HIDDEN], BF16)
         nc.scalar.dma_start(out=w2_rows[:], in_=tok_w2)
-        b1_rows = consts.tile([P, HIDDEN], BF16)
-        nw_rows = consts.tile([P, HIDDEN], BF16)
-        b2_rows = consts.tile([P, DETER], BF16)
-        nc.scalar.dma_start(out=nw_rows[:], in_=tok_nw.partition_broadcast(P))
-        nc.scalar.dma_start(out=b1_rows[:], in_=tok_b1.partition_broadcast(P))
-        nc.scalar.dma_start(out=b2_rows[:], in_=tok_b2.partition_broadcast(P))
 
         ident_f32 = consts.tile([P, P], F32)
         make_identity(nc, ident_f32[:])
@@ -89,6 +92,11 @@ def tile_mamba2backbone_pa_t_kernel(tc, stoch, action, tok_w1, tok_b1, tok_nw, t
         warm_out = consts.tile([P, 1], F32)
         nc.vector.memset(warm_in[:], 0.0)
         nc.scalar.activation(out=warm_out[:], in_=warm_in[:], func=ACT.Silu)
+
+        b1_bank = h_banks.tile([P, HIDDEN], F32, name="h")
+        nc.tensor.matmul(out=b1_bank[:], lhsT=ones[:], rhs=b1_row[:], start=True, stop=True)
+        b1_rows = consts.tile([P, HIDDEN], BF16)
+        nc.vector.tensor_copy(out=b1_rows[:], in_=b1_bank[:])
 
         w1_grouped = consts.tile([P, HIDDEN * PACK], BF16, align_bytes=64)
         w1_codes = consts.tile([P, HIDDEN], U32, align_bytes=64)
@@ -110,7 +118,13 @@ def tile_mamba2backbone_pa_t_kernel(tc, stoch, action, tok_w1, tok_b1, tok_nw, t
         nc.vector.quantize_mx(out=w2_codes[:].bitcast(FP8X4), scales=w2_scales[:], in_=w2_grouped[:])
 
         nw_bank = nw_banks.tile([P, HIDDEN], F32)
-        nc.tensor.matmul(out=nw_bank[:], lhsT=ident_bf16[:], rhs=nw_rows[:], start=True, stop=True)
+        nc.tensor.matmul(out=nw_bank[:], lhsT=ones[:], rhs=nw_b2_row[:, 0:HIDDEN], start=True, stop=True)
+        b2_bank = o_banks.tile([P, TILES, DETER], F32, name="o")
+        nc.tensor.matmul(
+            out=b2_bank[:, 0, :], lhsT=ones[:], rhs=nw_b2_row[:, HIDDEN : HIDDEN + DETER], start=True, stop=True
+        )
+        b2_rows = consts.tile([P, DETER], BF16)
+        nc.vector.tensor_copy(out=b2_rows[:], in_=b2_bank[:, 0, :])
 
         u_rows, u_bank, u_grouped, u_codes, u_scales = {}, {}, {}, {}, {}
         h, hb, rstd, zT, g_grouped, g_codes, g_scales, o = {}, {}, {}, {}, {}, {}, {}, {}

@@ -65,6 +65,11 @@ def tile_mamba2backbone_pa_t_kernel(tc, stoch, action, tok_w1, tok_b1, tok_nw, t
         nw_banks = ctx.enter_context(tc.psum_pool(name="nw_banks", bufs=1))
         ctx.enter_context(tc.manual_schedule())
 
+        w1_blocks = tok_w1.rearrange("(a b f) k -> a f b k", b=TILES, f=P)
+        w1_rows = []
+        for a in range(HIDDEN // GROUP):
+            w1_rows.append(consts.tile([P, TILES * K1], BF16, name="w1_rows%d" % a))
+            nc.sync.dma_start(out=w1_rows[a][:].rearrange("f (b k) -> f b k", b=TILES), in_=w1_blocks[a])
         b1_row = consts.tile([P, HIDDEN], BF16)
         nc.vector.memset(b1_row[:], 0.0)
         nc.sync.dma_start(out=b1_row[0:1, :], in_=tok_b1.unsqueeze(0))
@@ -74,11 +79,6 @@ def tile_mamba2backbone_pa_t_kernel(tc, stoch, action, tok_w1, tok_b1, tok_nw, t
         nc.vector.memset(nw_b2_row[:], 0.0)
         nc.scalar.dma_start(out=nw_b2_row[0:1, 0:HIDDEN], in_=tok_nw.unsqueeze(0))
         nc.scalar.dma_start(out=nw_b2_row[0:1, HIDDEN : HIDDEN + DETER], in_=tok_b2.unsqueeze(0))
-        w1_blocks = tok_w1.rearrange("(a b f) k -> a f b k", b=TILES, f=P)
-        w1_rows = []
-        for a in range(HIDDEN // GROUP):
-            w1_rows.append(consts.tile([P, TILES * K1], BF16, name="w1_rows%d" % a))
-            nc.sync.dma_start(out=w1_rows[a][:].rearrange("f (b k) -> f b k", b=TILES), in_=w1_blocks[a])
         w2_rows = consts.tile([P, HIDDEN], BF16)
         nc.scalar.dma_start(out=w2_rows[:], in_=tok_w2)
 
@@ -93,11 +93,6 @@ def tile_mamba2backbone_pa_t_kernel(tc, stoch, action, tok_w1, tok_b1, tok_nw, t
         nc.vector.memset(warm_in[:], 0.0)
         nc.scalar.activation(out=warm_out[:], in_=warm_in[:], func=ACT.Silu)
 
-        b1_bank = h_banks.tile([P, HIDDEN], F32, name="h")
-        nc.tensor.matmul(out=b1_bank[:], lhsT=ones[:], rhs=b1_row[:], start=True, stop=True)
-        b1_rows = consts.tile([P, HIDDEN], BF16)
-        nc.vector.tensor_copy(out=b1_rows[:], in_=b1_bank[:])
-
         w1_grouped = consts.tile([P, HIDDEN * PACK], BF16, align_bytes=64)
         w1_codes = consts.tile([P, HIDDEN], U32, align_bytes=64)
         w1_scales = consts.tile([P, HIDDEN], U8, align_bytes=64)
@@ -105,6 +100,11 @@ def tile_mamba2backbone_pa_t_kernel(tc, stoch, action, tok_w1, tok_b1, tok_nw, t
             w1_bank = transpose_words(nc, kT_banks, ident_f32[:], w1_rows[a][:])
             interleave_words(nc, w1_bank, w1_grouped[:].bitcast(F32)[:, a * GROUP * 2 : (a + 1) * GROUP * 2])
         nc.vector.quantize_mx(out=w1_codes[:].bitcast(FP8X4), scales=w1_scales[:], in_=w1_grouped[:])
+
+        b1_bank = h_banks.tile([P, HIDDEN], F32, name="h")
+        nc.tensor.matmul(out=b1_bank[:], lhsT=ones[:], rhs=b1_row[:], start=True, stop=True)
+        b1_rows = consts.tile([P, HIDDEN], BF16)
+        nc.vector.tensor_copy(out=b1_rows[:], in_=b1_bank[:])
 
         w2T = zT_banks.tile([P, PACK, DETER], BF16, tag="zT")
         for t in range(PACK):

@@ -20,6 +20,7 @@ EPS = 1e-4
 TILES = 2
 GROUP = TILES * P
 GROUPS = ROWS // GROUP
+PAIR = 2
 
 FLOPS = 2 * ROWS * K1 * HIDDEN + 2 * ROWS * HIDDEN * DETER
 
@@ -209,11 +210,12 @@ def tile_mamba2backbone_pa_t_kernel(tc, stoch, action, tok_w1, tok_b1, tok_nw, t
             nc.vector.quantize_mx(out=g_codes[g][:].bitcast(FP8X4), scales=g_scales[g][:], in_=g_grouped[g][:])
 
         def second_matmul(g):
-            o[g] = o_banks.tile([P, TILES, DETER], F32, name="o")
+            if g % PAIR == 0:
+                o[g // PAIR] = o_banks.tile([P, PAIR * TILES, DETER], F32, name="o")
             for i in range(TILES):
                 cols = slice(i * P, (i + 1) * P)
                 nc.tensor.matmul_mx(
-                    out=o[g][:, i, :],
+                    out=o[g // PAIR][:, (g % PAIR) * TILES + i, :],
                     lhsT=g_codes[g][:, cols].bitcast(FP8X4),
                     lhsT_scale=g_scales[g][:, cols],
                     rhs=w2_codes[:].bitcast(FP8X4),
@@ -223,12 +225,19 @@ def tile_mamba2backbone_pa_t_kernel(tc, stoch, action, tok_w1, tok_b1, tok_nw, t
                 )
 
         def store(g):
-            o_rows = packed.tile([P, TILES, DETER], F32)
+            if g % PAIR != PAIR - 1:
+                return
+            o_rows = packed.tile([P, PAIR * TILES, DETER], F32)
             nc.vector.tensor_tensor(
-                out=o_rows[:], in0=o[g][:], in1=b2_rows[:].unsqueeze(1).to_broadcast([P, TILES, DETER]), op=ALU.add
+                out=o_rows[:],
+                in0=o[g // PAIR][:],
+                in1=b2_rows[:].unsqueeze(1).to_broadcast([P, PAIR * TILES, DETER]),
+                op=ALU.add,
             )
+            first = (g // PAIR) * PAIR * GROUP
             nc.sync.dma_start(
-                out=out[g * GROUP : (g + 1) * GROUP, :].rearrange("(p i) d -> p i d", i=TILES), in_=o_rows[:]
+                out=out[first : first + PAIR * GROUP, :].rearrange("(a p i) d -> p a i d", a=PAIR, i=TILES),
+                in_=o_rows[:].rearrange("p (a i) d -> p a i d", a=PAIR),
             )
 
         def when_in_range(work, g):

import math
from contextlib import ExitStack

import concourse.mybir as mybir
from concourse.masks import make_identity

F32 = mybir.dt.float32
BF16 = mybir.dt.bfloat16
U32 = mybir.dt.uint32
U8 = mybir.dt.uint8
FP8X4 = mybir.dt.float8_e4m3fn_x4
ALU = mybir.AluOpType
ACT = mybir.ActivationFunctionType

P = 128
PACK = 4
ROWS, STOCH, ACTION, HIDDEN, DETER = 8192, 384, 128, 512, 128
K1 = STOCH + ACTION
EPS = 1e-4
TILES = 2
GROUP = TILES * P
GROUPS = ROWS // GROUP
PAIR = 2

FLOPS = 2 * ROWS * K1 * HIDDEN + 2 * ROWS * HIDDEN * DETER

LOAD_LEAD = 8
CLAMP_LEAD = 4
TRANSPOSE_U_LEAD = 3
EVACUATE_U_LEAD = 2
QUANTISE_U_LEAD = 2
MATMUL_1_LEAD = 1
NORMALISE_LAG = 2
SILU_LAG = NORMALISE_LAG + 1
QUANTISE_G_LAG = SILU_LAG + 1
MATMUL_2_LAG = QUANTISE_G_LAG + 1
STORE_LAG = MATMUL_2_LAG + 1


def transpose_words(nc, banks, ident_f32, rows):
    words = rows.bitcast(F32).rearrange("p (b w j) -> p b j w", b=TILES, j=2)
    bank = banks.tile([P, 2, TILES * P], F32, tag="kT")
    for b in range(TILES):
        for j in range(2):
            nc.tensor.transpose(bank[:, j, b * P : (b + 1) * P], words[:, b, j, :], ident_f32)
    return bank


def interleave_words(nc, bank, grouped_words):
    nc.scalar.copy(out=grouped_words.rearrange("q (c j) -> q c j", j=2), in_=bank[:].rearrange("q j c -> q c j"))


def tile_mamba2backbone_pa_t_kernel(tc, stoch, action, tok_w1, tok_b1, tok_nw, tok_w2, tok_b2, out):
    nc = tc.nc
    with ExitStack() as ctx:
        consts = ctx.enter_context(tc.tile_pool(name="consts", bufs=1))
        inputs = ctx.enter_context(tc.tile_pool(name="inputs", bufs=LOAD_LEAD))
        packed = ctx.enter_context(tc.tile_pool(name="packed", bufs=4))
        hidden_pool = ctx.enter_context(tc.tile_pool(name="hidden", bufs=(NORMALISE_LAG + 2) * TILES))
        scratch = ctx.enter_context(tc.tile_pool(name="scratch", bufs=4))
        columns = ctx.enter_context(tc.tile_pool(name="columns", bufs=NORMALISE_LAG + 3))
        kT_banks = ctx.enter_context(tc.psum_pool(name="kT_banks", bufs=2))
        h_banks = ctx.enter_context(tc.psum_pool(name="h_banks", bufs=TILES))
        zT_banks = ctx.enter_context(tc.psum_pool(name="zT_banks", bufs=TILES))
        o_banks = ctx.enter_context(tc.psum_pool(name="o_banks", bufs=1))
        nw_banks = ctx.enter_context(tc.psum_pool(name="nw_banks", bufs=1))
        ctx.enter_context(tc.manual_schedule())

        w1_blocks = tok_w1.rearrange("(a b f) k -> a f b k", b=TILES, f=P)
        w1_rows = []
        for a in range(HIDDEN // GROUP):
            w1_rows.append(consts.tile([P, TILES * K1], BF16, name="w1_rows%d" % a))
            nc.sync.dma_start(out=w1_rows[a][:].rearrange("f (b k) -> f b k", b=TILES), in_=w1_blocks[a])
        b1_row = consts.tile([P, HIDDEN], BF16)
        nc.vector.memset(b1_row[:], 0.0)
        nc.sync.dma_start(out=b1_row[0:1, :], in_=tok_b1.unsqueeze(0))
        ones = consts.tile([P, P], BF16)
        nc.vector.memset(ones[:], 1.0)
        nw_b2_row = consts.tile([P, HIDDEN + DETER], BF16)
        nc.vector.memset(nw_b2_row[:], 0.0)
        nc.scalar.dma_start(out=nw_b2_row[0:1, 0:HIDDEN], in_=tok_nw.unsqueeze(0))
        nc.scalar.dma_start(out=nw_b2_row[0:1, HIDDEN : HIDDEN + DETER], in_=tok_b2.unsqueeze(0))
        w2_rows = consts.tile([P, HIDDEN], BF16)
        nc.scalar.dma_start(out=w2_rows[:], in_=tok_w2)

        ident_f32 = consts.tile([P, P], F32)
        make_identity(nc, ident_f32[:])
        ident_bf16 = consts.tile([P, P], BF16)
        make_identity(nc, ident_bf16[:])
        minus_half = consts.tile([P, TILES], F32)
        nc.vector.memset(minus_half[:], -0.5)
        warm_in = consts.tile([P, 1], F32)
        warm_out = consts.tile([P, 1], F32)
        nc.vector.memset(warm_in[:], 0.0)
        nc.scalar.activation(out=warm_out[:], in_=warm_in[:], func=ACT.Silu)

        w1_grouped = consts.tile([P, HIDDEN * PACK], BF16, align_bytes=64)
        w1_codes = consts.tile([P, HIDDEN], U32, align_bytes=64)
        w1_scales = consts.tile([P, HIDDEN], U8, align_bytes=64)
        for a in range(HIDDEN // GROUP):
            w1_bank = transpose_words(nc, kT_banks, ident_f32[:], w1_rows[a][:])
            interleave_words(nc, w1_bank, w1_grouped[:].bitcast(F32)[:, a * GROUP * 2 : (a + 1) * GROUP * 2])
        nc.vector.quantize_mx(out=w1_codes[:].bitcast(FP8X4), scales=w1_scales[:], in_=w1_grouped[:])

        b1_bank = h_banks.tile([P, HIDDEN], F32, name="h")
        nc.tensor.matmul(out=b1_bank[:], lhsT=ones[:], rhs=b1_row[:], start=True, stop=True)
        b1_rows = consts.tile([P, HIDDEN], BF16)
        nc.vector.tensor_copy(out=b1_rows[:], in_=b1_bank[:])

        w2T = zT_banks.tile([P, PACK, DETER], BF16, tag="zT")
        for t in range(PACK):
            nc.tensor.transpose(w2T[:, t, :], w2_rows[:, t * P : (t + 1) * P], ident_bf16[:])
        w2_grouped = consts.tile([P, DETER * PACK], BF16, align_bytes=64)
        w2_codes = consts.tile([P, DETER], U32, align_bytes=64)
        w2_scales = consts.tile([P, DETER], U8, align_bytes=64)
        nc.vector.tensor_copy(
            out=w2_grouped[:].rearrange("q (d t) -> q d t", t=PACK), in_=w2T[:].rearrange("q t d -> q d t")
        )
        nc.vector.quantize_mx(out=w2_codes[:].bitcast(FP8X4), scales=w2_scales[:], in_=w2_grouped[:])

        nw_bank = nw_banks.tile([P, HIDDEN], F32)
        nc.tensor.matmul(out=nw_bank[:], lhsT=ones[:], rhs=nw_b2_row[:, 0:HIDDEN], start=True, stop=True)
        b2_bank = o_banks.tile([P, TILES, DETER], F32, name="o")
        nc.tensor.matmul(
            out=b2_bank[:, 0, :], lhsT=ones[:], rhs=nw_b2_row[:, HIDDEN : HIDDEN + DETER], start=True, stop=True
        )
        b2_rows = consts.tile([P, DETER], BF16)
        nc.vector.tensor_copy(out=b2_rows[:], in_=b2_bank[:, 0, :])

        u_rows, u_bank, u_grouped, u_codes, u_scales = {}, {}, {}, {}, {}
        h, hb, rstd, zT, g_grouped, g_codes, g_scales, o = {}, {}, {}, {}, {}, {}, {}, {}

        def load_u(g):
            u_rows[g] = inputs.tile([P, TILES * K1], BF16, name="u_rows")
            u_view = u_rows[g][:].rearrange("p (i k) -> p i k", i=TILES)
            rows = slice(g * GROUP, (g + 1) * GROUP)
            nc.sync.dma_start(out=u_view[:, :, 0:STOCH], in_=stoch[rows, :].rearrange("(p i) k -> p i k", i=TILES))
            nc.sync.dma_start(out=u_view[:, :, STOCH:K1], in_=action[rows, :].rearrange("(p i) k -> p i k", i=TILES))

        def clamp_action(g):
            an = u_rows[g][:].rearrange("p (i k) -> p i k", i=TILES)[:, :, STOCH:K1]
            nc.gpsimd.tensor_scalar(out=an, in0=an, scalar1=1.0, scalar2=-1.0, op0=ALU.min, op1=ALU.max)

        def transpose_u(g):
            u_bank[g] = transpose_words(nc, kT_banks, ident_f32[:], u_rows[g][:])

        def evacuate_u(g):
            u_grouped[g] = packed.tile([P, GROUP * PACK], BF16, align_bytes=64, name="u_grouped")
            interleave_words(nc, u_bank[g], u_grouped[g][:].bitcast(F32))

        def quantise_u(g):
            u_codes[g] = packed.tile([P, GROUP], U32, align_bytes=64, name="u_codes")
            u_scales[g] = packed.tile([P, GROUP], U8, align_bytes=64, name="u_scales")
            nc.vector.quantize_mx(out=u_codes[g][:].bitcast(FP8X4), scales=u_scales[g][:], in_=u_grouped[g][:])

        def first_matmul(g):
            for i in range(TILES):
                cols = slice(i * P, (i + 1) * P)
                h[g, i] = h_banks.tile([P, HIDDEN], F32, name="h")
                nc.tensor.matmul_mx(
                    out=h[g, i][:],
                    lhsT=u_codes[g][:, cols].bitcast(FP8X4),
                    lhsT_scale=u_scales[g][:, cols],
                    rhs=w1_codes[:].bitcast(FP8X4),
                    rhs_scale=w1_scales[:],
                    start=True,
                    stop=True,
                )

        def add_bias(g):
            for i in range(TILES):
                hb[g, i] = hidden_pool.tile([P, HIDDEN], F32, name="hb")
                nc.vector.tensor_tensor(out=hb[g, i][:], in0=h[g, i][:], in1=b1_rows[:], op=ALU.add)
            mean_sq = columns.tile([P, TILES], F32)
            for i in range(TILES):
                squares = scratch.tile([P, HIDDEN], BF16)
                nc.scalar.activation(
                    out=squares[:],
                    in_=hb[g, i][:],
                    func=ACT.Square,
                    scale=1.0 / math.sqrt(HIDDEN),
                    accum_out=mean_sq[:, i : i + 1],
                )
            shifted = columns.tile([P, TILES], F32)
            nc.gpsimd.tensor_scalar(out=shifted[:], in0=mean_sq[:], scalar1=EPS, scalar2=1.0, op0=ALU.add, op1=ALU.mult)
            rstd[g] = columns.tile([P, TILES], F32, name="rstd")
            nc.gpsimd.tensor_tensor(out=rstd[g][:], in0=shifted[:], in1=minus_half[:], op=ALU.pow)

        def normalise(g):
            for i in range(TILES):
                z = scratch.tile([P, HIDDEN], F32)
                nc.vector.scalar_tensor_tensor(
                    out=z[:], in0=hb[g, i][:], scalar=rstd[g][:, i : i + 1], in1=nw_bank[:], op0=ALU.mult, op1=ALU.mult
                )
                zT[g, i] = zT_banks.tile([P, PACK, P], F32, tag="zT", name="zT")
                for t in range(PACK):
                    nc.tensor.transpose(zT[g, i][:, t, :], z[:, t * P : (t + 1) * P], ident_f32[:])

        def silu(g):
            g_grouped[g] = packed.tile([P, GROUP * PACK], BF16, align_bytes=64, name="g_grouped")
            g_view = g_grouped[g][:].rearrange("q (r t) -> q r t", t=PACK)
            for i in range(TILES):
                nc.scalar.activation(
                    out=g_view[:, i * P : (i + 1) * P, :], in_=zT[g, i][:].rearrange("q t r -> q r t"), func=ACT.Silu
                )

        def quantise_g(g):
            g_codes[g] = packed.tile([P, GROUP], U32, align_bytes=64, name="g_codes")
            g_scales[g] = packed.tile([P, GROUP], U8, align_bytes=64, name="g_scales")
            nc.vector.quantize_mx(out=g_codes[g][:].bitcast(FP8X4), scales=g_scales[g][:], in_=g_grouped[g][:])

        def second_matmul(g):
            if g % PAIR == 0:
                o[g // PAIR] = o_banks.tile([P, PAIR * TILES, DETER], F32, name="o")
            for i in range(TILES):
                cols = slice(i * P, (i + 1) * P)
                nc.tensor.matmul_mx(
                    out=o[g // PAIR][:, (g % PAIR) * TILES + i, :],
                    lhsT=g_codes[g][:, cols].bitcast(FP8X4),
                    lhsT_scale=g_scales[g][:, cols],
                    rhs=w2_codes[:].bitcast(FP8X4),
                    rhs_scale=w2_scales[:],
                    start=True,
                    stop=True,
                )

        def store(g):
            if g % PAIR != PAIR - 1:
                return
            o_rows = packed.tile([P, PAIR * TILES, DETER], F32)
            nc.vector.tensor_tensor(
                out=o_rows[:],
                in0=o[g // PAIR][:],
                in1=b2_rows[:].unsqueeze(1).to_broadcast([P, PAIR * TILES, DETER]),
                op=ALU.add,
            )
            first = (g // PAIR) * PAIR * GROUP
            nc.sync.dma_start(
                out=out[first : first + PAIR * GROUP, :].rearrange("(a p i) d -> p a i d", a=PAIR, i=TILES),
                in_=o_rows[:].rearrange("p (a i) d -> p a i d", a=PAIR),
            )

        def when_in_range(work, g):
            if 0 <= g < GROUPS:
                work(g)

        for s in range(-LOAD_LEAD, GROUPS + STORE_LAG):
            when_in_range(load_u, s + LOAD_LEAD)
            when_in_range(clamp_action, s + CLAMP_LEAD)
            when_in_range(transpose_u, s + TRANSPOSE_U_LEAD)
            when_in_range(evacuate_u, s + EVACUATE_U_LEAD)
            when_in_range(silu, s - SILU_LAG)
            when_in_range(store, s - STORE_LAG)
            when_in_range(second_matmul, s - MATMUL_2_LAG)
            when_in_range(add_bias, s)
            when_in_range(first_matmul, s + MATMUL_1_LEAD)
            when_in_range(normalise, s - NORMALISE_LAG)
            when_in_range(quantise_u, s + QUANTISE_U_LEAD)
            when_in_range(quantise_g, s - QUANTISE_G_LAG)
